import numpy as np
import ml_dtypes

BF16 = ml_dtypes.bfloat16


def bf(x):
    return np.asarray(x, np.float32).astype(BF16)


def f32(x):
    return np.asarray(x, np.float32)


def f64(x):
    return np.asarray(x).astype(np.float64)


def striped(idx):
    return np.tile(idx.reshape(-1, 16).T, (8, 1))


S, D, K, E, O, N = 512, 128, 4, 64, 128, 256


def setup_inputs():
    return {"table": bf(np.random.standard_normal((S, D))), "w1": bf(np.random.standard_normal((K * D, D)) / np.sqrt(K * D)), "b1": f32(0.1 * np.random.standard_normal((D, 1))), "wc": bf(np.random.standard_normal((D, O)) / np.sqrt(D)), "offs": striped(np.random.permutation(S)[:N])}


def reference(table, w1, b1, wc, offs):
    idx = offs[:16].T.reshape(-1)
    picked = f64(table)[idx].T.reshape(D, K, E)
    hid = np.maximum(np.einsum("tfd,ftn->dn", f64(w1).reshape(K, D, D), picked) + f64(b1), 0.0)
    edge = (1.0 / K) * np.einsum("fo,ftn->on", f64(wc), picked)
    return np.concatenate([hid, edge], axis=0)

@@ -1,0 +1,57 @@
+import concourse.mybir as mybir
+from concourse.masks import make_identity
+
+P = 128
+NODES = 512
+MEMBERS = 4
+EDGES = 64
+BLOCKS = NODES // P
+LIST_COLUMNS = EDGES // 16
+
+BF16, F32, U16 = mybir.dt.bfloat16, mybir.dt.float32, mybir.dt.uint16
+
+FLOPS = 2 * (2 * P * P * MEMBERS * EDGES)
+
+
+def tile_hypergraphcompressor_kernel(tc, table, w1, b1, wc, offs, out):
+    nc = tc.nc
+    with (
+        tc.tile_pool(name="held", bufs=1) as held,
+        tc.psum_pool(name="psum", bufs=1) as psum,
+    ):
+        offsets = held.tile([P, MEMBERS * LIST_COLUMNS], U16, name="offsets")
+        nc.sync.dma_start(offsets[:], offs)
+
+        rows = held.tile([P, BLOCKS, P], BF16, name="rows")
+        nc.sync.dma_start(rows[:], table.rearrange("(c p) f -> p c f", p=P))
+
+        w1_sb = held.tile([P, MEMBERS, P], BF16, name="w1_sb")
+        nc.scalar.dma_start(w1_sb[:], w1.rearrange("(t f) d -> f t d", f=P))
+        wc_sb = held.tile([P, P], BF16, name="wc_sb")
+        nc.scalar.dma_start(wc_sb[:], wc)
+        b1_sb = held.tile([P, 1], F32, name="b1_sb")
+        nc.scalar.dma_start(b1_sb[:], b1)
+
+        identity = held.tile([P, P], BF16, name="identity")
+        make_identity(nc, identity[:])
+        flipped = psum.tile([P, NODES], BF16, name="flipped")
+        for c in range(BLOCKS):
+            nc.tensor.transpose(flipped[:, c * P : (c + 1) * P], rows[:, c, :], identity[:])
+        nodes = held.tile([P, NODES], BF16, name="nodes")
+        nc.vector.tensor_copy(nodes[:], flipped[:])
+
+        hid_ps = psum.tile([P, EDGES], F32, name="hid_ps")
+        edge_ps = psum.tile([P, EDGES], F32, name="edge_ps")
+        for t in range(MEMBERS):
+            member = nodes[:].indirect(offsets[:, t * LIST_COLUMNS : (t + 1) * LIST_COLUMNS])
+            nc.tensor.matmul(hid_ps[:], w1_sb[:, t, :], member, start=(t == 0), stop=(t == MEMBERS - 1))
+        for t in range(MEMBERS):
+            member = nodes[:].indirect(offsets[:, t * LIST_COLUMNS : (t + 1) * LIST_COLUMNS])
+            nc.tensor.matmul(edge_ps[:], wc_sb[:], member, start=(t == 0), stop=(t == MEMBERS - 1))
+
+        hid_sb = held.tile([P, EDGES], F32, name="hid_sb")
+        nc.scalar.activation(hid_sb[:], hid_ps[:], mybir.ActivationFunctionType.Relu, bias=b1_sb[:], scale=1.0)
+        nc.sync.dma_start(out[0:P, :], hid_sb[:])
+        edge_sb = held.tile([P, EDGES], F32, name="edge_sb")
+        nc.vector.tensor_scalar_mul(edge_sb[:], edge_ps[:], 1.0 / MEMBERS)
+        nc.scalar.dma_start(out[P : 2 * P, :], edge_sb[:])

@@ -18,27 +18,30 @@ def tile_hypergraphcompressor_kernel(tc, table, w1, b1, wc, offs, out):
     with (
         tc.tile_pool(name="held", bufs=1) as held,
         tc.psum_pool(name="psum", bufs=1) as psum,
+        tc.psum_pool(name="flip", bufs=2) as flip,
     ):
+        rows = held.tile([P, BLOCKS, P], BF16, name="rows")
+        for c in range(BLOCKS):
+            queue = nc.sync if c % 2 == 0 else nc.scalar
+            queue.dma_start(rows[:, c, :], table[c * P : (c + 1) * P, :])
+
         offsets = held.tile([P, MEMBERS * LIST_COLUMNS], U16, name="offsets")
         nc.sync.dma_start(offsets[:], offs)
-
-        rows = held.tile([P, BLOCKS, P], BF16, name="rows")
-        nc.sync.dma_start(rows[:], table.rearrange("(c p) f -> p c f", p=P))
 
         w1_sb = held.tile([P, MEMBERS, P], BF16, name="w1_sb")
         nc.scalar.dma_start(w1_sb[:], w1.rearrange("(t f) d -> f t d", f=P))
         wc_sb = held.tile([P, P], BF16, name="wc_sb")
-        nc.scalar.dma_start(wc_sb[:], wc)
+        nc.sync.dma_start(wc_sb[:], wc)
         b1_sb = held.tile([P, 1], F32, name="b1_sb")
         nc.scalar.dma_start(b1_sb[:], b1)
 
         identity = held.tile([P, P], BF16, name="identity")
         make_identity(nc, identity[:])
-        flipped = psum.tile([P, NODES], BF16, name="flipped")
-        for c in range(BLOCKS):
-            nc.tensor.transpose(flipped[:, c * P : (c + 1) * P], rows[:, c, :], identity[:])
         nodes = held.tile([P, NODES], BF16, name="nodes")
-        nc.vector.tensor_copy(nodes[:], flipped[:])
+        for c in range(BLOCKS):
+            flipped = flip.tile([P, P], BF16, name="flipped")
+            nc.tensor.transpose(flipped[:], rows[:, c, :], identity[:])
+            nc.vector.tensor_copy(nodes[:, c * P : (c + 1) * P], flipped[:])
 
         hid_ps = psum.tile([P, EDGES], F32, name="hid_ps")
         edge_ps = psum.tile([P, EDGES], F32, name="edge_ps")

@@ -28,12 +28,12 @@ def tile_hypergraphcompressor_kernel(tc, table, w1, b1, wc, offs, out):
         offsets = held.tile([P, MEMBERS * LIST_COLUMNS], U16, name="offsets")
         nc.sync.dma_start(offsets[:], offs)
 
-        w1_sb = held.tile([P, MEMBERS, P], BF16, name="w1_sb")
-        nc.scalar.dma_start(w1_sb[:], w1.rearrange("(t f) d -> f t d", f=P))
         wc_sb = held.tile([P, P], BF16, name="wc_sb")
         nc.sync.dma_start(wc_sb[:], wc)
         b1_sb = held.tile([P, 1], F32, name="b1_sb")
         nc.scalar.dma_start(b1_sb[:], b1)
+        w1_sb = held.tile([P, MEMBERS, P], BF16, name="w1_sb")
+        nc.scalar.dma_start(w1_sb[:], w1.rearrange("(t f) d -> f t d", f=P))
 
         identity = held.tile([P, P], BF16, name="identity")
         make_identity(nc, identity[:])
@@ -47,14 +47,14 @@ def tile_hypergraphcompressor_kernel(tc, table, w1, b1, wc, offs, out):
         edge_ps = psum.tile([P, EDGES], F32, name="edge_ps")
         for t in range(MEMBERS):
             member = nodes[:].indirect(offsets[:, t * LIST_COLUMNS : (t + 1) * LIST_COLUMNS])
-            nc.tensor.matmul(hid_ps[:], w1_sb[:, t, :], member, start=(t == 0), stop=(t == MEMBERS - 1))
+            nc.tensor.matmul(edge_ps[:], wc_sb[:], member, start=(t == 0), stop=(t == MEMBERS - 1))
         for t in range(MEMBERS):
             member = nodes[:].indirect(offsets[:, t * LIST_COLUMNS : (t + 1) * LIST_COLUMNS])
-            nc.tensor.matmul(edge_ps[:], wc_sb[:], member, start=(t == 0), stop=(t == MEMBERS - 1))
+            nc.tensor.matmul(hid_ps[:], w1_sb[:, t, :], member, start=(t == 0), stop=(t == MEMBERS - 1))
 
-        hid_sb = held.tile([P, EDGES], F32, name="hid_sb")
-        nc.scalar.activation(hid_sb[:], hid_ps[:], mybir.ActivationFunctionType.Relu, bias=b1_sb[:], scale=1.0)
-        nc.sync.dma_start(out[0:P, :], hid_sb[:])
         edge_sb = held.tile([P, EDGES], F32, name="edge_sb")
         nc.vector.tensor_scalar_mul(edge_sb[:], edge_ps[:], 1.0 / MEMBERS)
-        nc.scalar.dma_start(out[P : 2 * P, :], edge_sb[:])
+        nc.sync.dma_start(out[P : 2 * P, :], edge_sb[:])
+        hid_sb = held.tile([P, EDGES], F32, name="hid_sb")
+        nc.vector.tensor_scalar(hid_sb[:], hid_ps[:], b1_sb[:], 0.0, mybir.AluOpType.add, mybir.AluOpType.max)
+        nc.scalar.dma_start(out[0:P, :], hid_sb[:])

@@ -8,6 +8,9 @@ EDGES = 64
 BLOCKS = NODES // P
 LIST_COLUMNS = EDGES // 16
 
+FILL_BEFORE = 3
+FILL_AFTER = 1
+
 BF16, F32, U16 = mybir.dt.bfloat16, mybir.dt.float32, mybir.dt.uint16
 
 FLOPS = 2 * (2 * P * P * MEMBERS * EDGES)
@@ -35,6 +38,18 @@ def tile_hypergraphcompressor_kernel(tc, table, w1, b1, wc, offs, out):
         w1_sb = held.tile([P, MEMBERS, P], BF16, name="w1_sb")
         nc.scalar.dma_start(w1_sb[:], w1.rearrange("(t f) d -> f t d", f=P))
 
+        zeros = held.tile([P, P], BF16, name="zeros")
+        nc.gpsimd.memset(zeros[:], 0.0)
+        idle_ps = psum.tile([P, BLOCKS, P], F32, name="idle_ps")
+
+        def keep_busy(count):
+            for i in range(count):
+                nc.tensor.matmul(
+                    idle_ps[:], zeros[:], zeros[:].unsqueeze(1).to_broadcast([P, BLOCKS, P]), start=True, stop=True
+                )
+
+        keep_busy(FILL_BEFORE)
+
         identity = held.tile([P, P], BF16, name="identity")
         make_identity(nc, identity[:])
         nodes = held.tile([P, NODES], BF16, name="nodes")
@@ -42,6 +57,7 @@ def tile_hypergraphcompressor_kernel(tc, table, w1, b1, wc, offs, out):
             flipped = flip.tile([P, P], BF16, name="flipped")
             nc.tensor.transpose(flipped[:], rows[:, c, :], identity[:])
             nc.vector.tensor_copy(nodes[:, c * P : (c + 1) * P], flipped[:])
+        keep_busy(FILL_AFTER)
 
         hid_ps = psum.tile([P, EDGES], F32, name="hid_ps")
         edge_ps = psum.tile([P, EDGES], F32, name="edge_ps")

@@ -8,9 +8,6 @@ EDGES = 64
 BLOCKS = NODES // P
 LIST_COLUMNS = EDGES // 16
 
-FILL_BEFORE = 3
-FILL_AFTER = 1
-
 BF16, F32, U16 = mybir.dt.bfloat16, mybir.dt.float32, mybir.dt.uint16
 
 FLOPS = 2 * (2 * P * P * MEMBERS * EDGES)
@@ -38,18 +35,6 @@ def tile_hypergraphcompressor_kernel(tc, table, w1, b1, wc, offs, out):
         w1_sb = held.tile([P, MEMBERS, P], BF16, name="w1_sb")
         nc.scalar.dma_start(w1_sb[:], w1.rearrange("(t f) d -> f t d", f=P))
 
-        zeros = held.tile([P, P], BF16, name="zeros")
-        nc.gpsimd.memset(zeros[:], 0.0)
-        idle_ps = psum.tile([P, BLOCKS, P], F32, name="idle_ps")
-
-        def keep_busy(count):
-            for i in range(count):
-                nc.tensor.matmul(
-                    idle_ps[:], zeros[:], zeros[:].unsqueeze(1).to_broadcast([P, BLOCKS, P]), start=True, stop=True
-                )
-
-        keep_busy(FILL_BEFORE)
-
         identity = held.tile([P, P], BF16, name="identity")
         make_identity(nc, identity[:])
         nodes = held.tile([P, NODES], BF16, name="nodes")
@@ -57,19 +42,21 @@ def tile_hypergraphcompressor_kernel(tc, table, w1, b1, wc, offs, out):
             flipped = flip.tile([P, P], BF16, name="flipped")
             nc.tensor.transpose(flipped[:], rows[:, c, :], identity[:])
             nc.vector.tensor_copy(nodes[:, c * P : (c + 1) * P], flipped[:])
-        keep_busy(FILL_AFTER)
+
+        edge_ps = psum.tile([P, MEMBERS * EDGES], F32, name="edge_ps")
+        nc.tensor.matmul(edge_ps[:], wc_sb[:], nodes[:].indirect(offsets[:]), start=True, stop=True)
 
         hid_ps = psum.tile([P, EDGES], F32, name="hid_ps")
-        edge_ps = psum.tile([P, EDGES], F32, name="edge_ps")
-        for t in range(MEMBERS):
-            member = nodes[:].indirect(offsets[:, t * LIST_COLUMNS : (t + 1) * LIST_COLUMNS])
-            nc.tensor.matmul(edge_ps[:], wc_sb[:], member, start=(t == 0), stop=(t == MEMBERS - 1))
         for t in range(MEMBERS):
             member = nodes[:].indirect(offsets[:, t * LIST_COLUMNS : (t + 1) * LIST_COLUMNS])
             nc.tensor.matmul(hid_ps[:], w1_sb[:, t, :], member, start=(t == 0), stop=(t == MEMBERS - 1))
 
+        edge_sum = held.tile([P, EDGES], F32, name="edge_sum")
+        nc.vector.tensor_reduce(
+            edge_sum[:], edge_ps[:].rearrange("p (t n) -> p n t", t=MEMBERS), mybir.AxisListType.X, mybir.AluOpType.add
+        )
         edge_sb = held.tile([P, EDGES], F32, name="edge_sb")
-        nc.vector.tensor_scalar_mul(edge_sb[:], edge_ps[:], 1.0 / MEMBERS)
+        nc.vector.tensor_scalar_mul(edge_sb[:], edge_sum[:], 1.0 / MEMBERS)
         nc.sync.dma_start(out[P : 2 * P, :], edge_sb[:])
         hid_sb = held.tile([P, EDGES], F32, name="hid_sb")
         nc.vector.tensor_scalar(hid_sb[:], hid_ps[:], b1_sb[:], 0.0, mybir.AluOpType.add, mybir.AluOpType.max)

@@ -18,12 +18,9 @@ def tile_hypergraphcompressor_kernel(tc, table, w1, b1, wc, offs, out):
     with (
         tc.tile_pool(name="held", bufs=1) as held,
         tc.psum_pool(name="psum", bufs=1) as psum,
-        tc.psum_pool(name="flip", bufs=2) as flip,
     ):
         rows = held.tile([P, BLOCKS, P], BF16, name="rows")
-        for c in range(BLOCKS):
-            queue = nc.sync if c % 2 == 0 else nc.scalar
-            queue.dma_start(rows[:, c, :], table[c * P : (c + 1) * P, :])
+        nc.sync.dma_start(rows[:], table.rearrange("(c p) f -> p c f", p=P))
 
         offsets = held.tile([P, MEMBERS * LIST_COLUMNS], U16, name="offsets")
         nc.sync.dma_start(offsets[:], offs)
@@ -37,26 +34,23 @@ def tile_hypergraphcompressor_kernel(tc, table, w1, b1, wc, offs, out):
 
         identity = held.tile([P, P], BF16, name="identity")
         make_identity(nc, identity[:])
-        nodes = held.tile([P, NODES], BF16, name="nodes")
+        flipped = psum.tile([P, NODES], BF16, name="flipped")
         for c in range(BLOCKS):
-            flipped = flip.tile([P, P], BF16, name="flipped")
-            nc.tensor.transpose(flipped[:], rows[:, c, :], identity[:])
-            nc.vector.tensor_copy(nodes[:, c * P : (c + 1) * P], flipped[:])
-
-        edge_ps = psum.tile([P, MEMBERS * EDGES], F32, name="edge_ps")
-        nc.tensor.matmul(edge_ps[:], wc_sb[:], nodes[:].indirect(offsets[:]), start=True, stop=True)
+            nc.tensor.transpose(flipped[:, c * P : (c + 1) * P], rows[:, c, :], identity[:])
+        nodes = held.tile([P, NODES], BF16, name="nodes")
+        nc.vector.tensor_copy(nodes[:], flipped[:])
 
         hid_ps = psum.tile([P, EDGES], F32, name="hid_ps")
+        edge_ps = psum.tile([P, EDGES], F32, name="edge_ps")
+        for t in range(MEMBERS):
+            member = nodes[:].indirect(offsets[:, t * LIST_COLUMNS : (t + 1) * LIST_COLUMNS])
+            nc.tensor.matmul(edge_ps[:], wc_sb[:], member, start=(t == 0), stop=(t == MEMBERS - 1))
         for t in range(MEMBERS):
             member = nodes[:].indirect(offsets[:, t * LIST_COLUMNS : (t + 1) * LIST_COLUMNS])
             nc.tensor.matmul(hid_ps[:], w1_sb[:, t, :], member, start=(t == 0), stop=(t == MEMBERS - 1))
 
-        edge_sum = held.tile([P, EDGES], F32, name="edge_sum")
-        nc.vector.tensor_reduce(
-            edge_sum[:], edge_ps[:].rearrange("p (t n) -> p n t", t=MEMBERS), mybir.AxisListType.X, mybir.AluOpType.add
-        )
         edge_sb = held.tile([P, EDGES], F32, name="edge_sb")
-        nc.vector.tensor_scalar_mul(edge_sb[:], edge_sum[:], 1.0 / MEMBERS)
+        nc.vector.tensor_scalar_mul(edge_sb[:], edge_ps[:], 1.0 / MEMBERS)
         nc.sync.dma_start(out[P : 2 * P, :], edge_sb[:])
         hid_sb = held.tile([P, EDGES], F32, name="hid_sb")
         nc.vector.tensor_scalar(hid_sb[:], hid_ps[:], b1_sb[:], 0.0, mybir.AluOpType.add, mybir.AluOpType.max)

@@ -20,7 +20,9 @@ def tile_hypergraphcompressor_kernel(tc, table, w1, b1, wc, offs, out):
         tc.psum_pool(name="psum", bufs=1) as psum,
     ):
         rows = held.tile([P, BLOCKS, P], BF16, name="rows")
-        nc.sync.dma_start(rows[:], table.rearrange("(c p) f -> p c f", p=P))
+        for c in range(BLOCKS):
+            queue = nc.sync if c % 2 == 0 else nc.scalar
+            queue.dma_start(rows[:, c, :], table[c * P : (c + 1) * P, :])
 
         offsets = held.tile([P, MEMBERS * LIST_COLUMNS], U16, name="offsets")
         nc.sync.dma_start(offsets[:], offs)

@@ -20,19 +20,20 @@ def tile_hypergraphcompressor_kernel(tc, table, w1, b1, wc, offs, out):
         tc.psum_pool(name="psum", bufs=1) as psum,
     ):
         rows = held.tile([P, BLOCKS, P], BF16, name="rows")
-        for c in range(BLOCKS):
-            queue = nc.sync if c % 2 == 0 else nc.scalar
-            queue.dma_start(rows[:, c, :], table[c * P : (c + 1) * P, :])
+        blocks = table.rearrange("(c p) f -> p c f", p=P)
+        half = BLOCKS // 2
+        nc.sync.dma_start(rows[:, 0:half, :], blocks[:, 0:half, :])
+        nc.scalar.dma_start(rows[:, half:BLOCKS, :], blocks[:, half:BLOCKS, :])
 
         offsets = held.tile([P, MEMBERS * LIST_COLUMNS], U16, name="offsets")
         nc.sync.dma_start(offsets[:], offs)
 
         wc_sb = held.tile([P, P], BF16, name="wc_sb")
         nc.sync.dma_start(wc_sb[:], wc)
-        b1_sb = held.tile([P, 1], F32, name="b1_sb")
-        nc.scalar.dma_start(b1_sb[:], b1)
         w1_sb = held.tile([P, MEMBERS, P], BF16, name="w1_sb")
         nc.scalar.dma_start(w1_sb[:], w1.rearrange("(t f) d -> f t d", f=P))
+        b1_sb = held.tile([P, 1], F32, name="b1_sb")
+        nc.scalar.dma_start(b1_sb[:], b1)
 
         identity = held.tile([P, P], BF16, name="identity")
         make_identity(nc, identity[:])

@@ -37,11 +37,12 @@ def tile_hypergraphcompressor_kernel(tc, table, w1, b1, wc, offs, out):
 
         identity = held.tile([P, P], BF16, name="identity")
         make_identity(nc, identity[:])
-        flipped = psum.tile([P, NODES], BF16, name="flipped")
-        for c in range(BLOCKS):
-            nc.tensor.transpose(flipped[:, c * P : (c + 1) * P], rows[:, c, :], identity[:])
         nodes = held.tile([P, NODES], BF16, name="nodes")
-        nc.vector.tensor_copy(nodes[:], flipped[:])
+        for h in range(2):
+            flipped = psum.tile([P, half * P], BF16, name="flipped%d" % h)
+            for c in range(half):
+                nc.tensor.transpose(flipped[:, c * P : (c + 1) * P], rows[:, h * half + c, :], identity[:])
+            nc.vector.tensor_copy(nodes[:, h * half * P : (h + 1) * half * P], flipped[:])
 
         hid_ps = psum.tile([P, EDGES], F32, name="hid_ps")
         edge_ps = psum.tile([P, EDGES], F32, name="edge_ps")

@@ -44,17 +44,17 @@ def tile_hypergraphcompressor_kernel(tc, table, w1, b1, wc, offs, out):
                 nc.tensor.transpose(flipped[:, c * P : (c + 1) * P], rows[:, h * half + c, :], identity[:])
             nc.vector.tensor_copy(nodes[:, h * half * P : (h + 1) * half * P], flipped[:])
 
+        edge_ps = psum.tile([P, MEMBERS, EDGES], F32, name="edge_ps")
+        nc.tensor.matmul(edge_ps[:].rearrange("p t n -> p (t n)"), wc_sb[:], nodes[:].indirect(offsets[:]), start=True, stop=True)
         hid_ps = psum.tile([P, EDGES], F32, name="hid_ps")
-        edge_ps = psum.tile([P, EDGES], F32, name="edge_ps")
-        for t in range(MEMBERS):
-            member = nodes[:].indirect(offsets[:, t * LIST_COLUMNS : (t + 1) * LIST_COLUMNS])
-            nc.tensor.matmul(edge_ps[:], wc_sb[:], member, start=(t == 0), stop=(t == MEMBERS - 1))
         for t in range(MEMBERS):
             member = nodes[:].indirect(offsets[:, t * LIST_COLUMNS : (t + 1) * LIST_COLUMNS])
             nc.tensor.matmul(hid_ps[:], w1_sb[:, t, :], member, start=(t == 0), stop=(t == MEMBERS - 1))
 
+        edge_sum = held.tile([P, EDGES], F32, name="edge_sum")
+        nc.vector.tensor_reduce(edge_sum[:], edge_ps[:].rearrange("p t n -> p n t"), mybir.AxisListType.X, mybir.AluOpType.add)
         edge_sb = held.tile([P, EDGES], F32, name="edge_sb")
-        nc.vector.tensor_scalar_mul(edge_sb[:], edge_ps[:], 1.0 / MEMBERS)
+        nc.vector.tensor_scalar_mul(edge_sb[:], edge_sum[:], 1.0 / MEMBERS)
         nc.sync.dma_start(out[P : 2 * P, :], edge_sb[:])
         hid_sb = held.tile([P, EDGES], F32, name="hid_sb")
         nc.vector.tensor_scalar(hid_sb[:], hid_ps[:], b1_sb[:], 0.0, mybir.AluOpType.add, mybir.AluOpType.max)

@@ -38,11 +38,10 @@ def tile_hypergraphcompressor_kernel(tc, table, w1, b1, wc, offs, out):
         identity = held.tile([P, P], BF16, name="identity")
         make_identity(nc, identity[:])
         nodes = held.tile([P, NODES], BF16, name="nodes")
-        for h in range(2):
-            flipped = psum.tile([P, half * P], BF16, name="flipped%d" % h)
-            for c in range(half):
-                nc.tensor.transpose(flipped[:, c * P : (c + 1) * P], rows[:, h * half + c, :], identity[:])
-            nc.vector.tensor_copy(nodes[:, h * half * P : (h + 1) * half * P], flipped[:])
+        for c in range(BLOCKS):
+            flipped = psum.tile([P, P], BF16, name="flipped%d" % c)
+            nc.tensor.transpose(flipped[:], rows[:, c, :], identity[:])
+            nc.vector.tensor_copy(nodes[:, c * P : (c + 1) * P], flipped[:])
 
         edge_ps = psum.tile([P, MEMBERS, EDGES], F32, name="edge_ps")
         nc.tensor.matmul(edge_ps[:].rearrange("p t n -> p (t n)"), wc_sb[:], nodes[:].indirect(offsets[:]), start=True, stop=True)

@@ -36,7 +36,8 @@ def tile_hypergraphcompressor_kernel(tc, table, w1, b1, wc, offs, out):
         nc.scalar.dma_start(b1_sb[:], b1)
 
         identity = held.tile([P, P], BF16, name="identity")
-        make_identity(nc, identity[:])
+        nc.vector.memset(identity[:], 0.0)
+        make_identity(nc, identity[:], nomemset=True)
         nodes = held.tile([P, NODES], BF16, name="nodes")
         for c in range(BLOCKS):
             flipped = psum.tile([P, P], BF16, name="flipped%d" % c)
@@ -54,7 +55,7 @@ def tile_hypergraphcompressor_kernel(tc, table, w1, b1, wc, offs, out):
         nc.vector.tensor_reduce(edge_sum[:], edge_ps[:].rearrange("p t n -> p n t"), mybir.AxisListType.X, mybir.AluOpType.add)
         edge_sb = held.tile([P, EDGES], F32, name="edge_sb")
         nc.vector.tensor_scalar_mul(edge_sb[:], edge_sum[:], 1.0 / MEMBERS)
-        nc.sync.dma_start(out[P : 2 * P, :], edge_sb[:])
+        nc.scalar.dma_start(out[P : 2 * P, :], edge_sb[:])
         hid_sb = held.tile([P, EDGES], F32, name="hid_sb")
         nc.vector.tensor_scalar(hid_sb[:], hid_ps[:], b1_sb[:], 0.0, mybir.AluOpType.add, mybir.AluOpType.max)
-        nc.scalar.dma_start(out[0:P, :], hid_sb[:])
+        nc.sync.dma_start(out[0:P, :], hid_sb[:])

@@ -29,9 +29,9 @@ def tile_hypergraphcompressor_kernel(tc, table, w1, b1, wc, offs, out):
         nc.sync.dma_start(offsets[:], offs)
 
         wc_sb = held.tile([P, P], BF16, name="wc_sb")
-        nc.sync.dma_start(wc_sb[:], wc)
+        nc.scalar.dma_start(wc_sb[:], wc)
         w1_sb = held.tile([P, MEMBERS, P], BF16, name="w1_sb")
-        nc.scalar.dma_start(w1_sb[:], w1.rearrange("(t f) d -> f t d", f=P))
+        nc.sync.dma_start(w1_sb[:], w1.rearrange("(t f) d -> f t d", f=P))
         b1_sb = held.tile([P, 1], F32, name="b1_sb")
         nc.scalar.dma_start(b1_sb[:], b1)
 

@@ -36,8 +36,12 @@ def tile_hypergraphcompressor_kernel(tc, table, w1, b1, wc, offs, out):
         nc.scalar.dma_start(b1_sb[:], b1)
 
         identity = held.tile([P, P], BF16, name="identity")
+        zero = held.tile([P, 1], F32, name="zero")
+        nc.vector.memset(zero[:], 0.0)
         nc.vector.memset(identity[:], 0.0)
         make_identity(nc, identity[:], nomemset=True)
+        early = held.tile([P, 1], F32, name="early")
+        nc.scalar.activation(early[:], zero[:], mybir.ActivationFunctionType.Relu)
         nodes = held.tile([P, NODES], BF16, name="nodes")
         for c in range(BLOCKS):
             flipped = psum.tile([P, P], BF16, name="flipped%d" % c)
@@ -55,7 +59,7 @@ def tile_hypergraphcompressor_kernel(tc, table, w1, b1, wc, offs, out):
         nc.vector.tensor_reduce(edge_sum[:], edge_ps[:].rearrange("p t n -> p n t"), mybir.AxisListType.X, mybir.AluOpType.add)
         edge_sb = held.tile([P, EDGES], F32, name="edge_sb")
         nc.vector.tensor_scalar_mul(edge_sb[:], edge_sum[:], 1.0 / MEMBERS)
-        nc.scalar.dma_start(out[P : 2 * P, :], edge_sb[:])
+        nc.sync.dma_start(out[P : 2 * P, :], edge_sb[:])
         hid_sb = held.tile([P, EDGES], F32, name="hid_sb")
-        nc.vector.tensor_scalar(hid_sb[:], hid_ps[:], b1_sb[:], 0.0, mybir.AluOpType.add, mybir.AluOpType.max)
-        nc.sync.dma_start(out[0:P, :], hid_sb[:])
+        nc.scalar.activation(hid_sb[:], hid_ps[:], mybir.ActivationFunctionType.Relu, bias=b1_sb[:])
+        nc.scalar.dma_start(out[0:P, :], hid_sb[:])

@@ -48,8 +48,10 @@ def tile_hypergraphcompressor_kernel(tc, table, w1, b1, wc, offs, out):
             nc.tensor.transpose(flipped[:], rows[:, c, :], identity[:])
             nc.vector.tensor_copy(nodes[:, c * P : (c + 1) * P], flipped[:])
 
-        edge_ps = psum.tile([P, MEMBERS, EDGES], F32, name="edge_ps")
-        nc.tensor.matmul(edge_ps[:].rearrange("p t n -> p (t n)"), wc_sb[:], nodes[:].indirect(offsets[:]), start=True, stop=True)
+        edge_ps = psum.tile([P, 2, EDGES], F32, name="edge_ps")
+        for h in range(2):
+            two_members = nodes[:].indirect(offsets[:, 2 * h * LIST_COLUMNS : 2 * (h + 1) * LIST_COLUMNS])
+            nc.tensor.matmul(edge_ps[:].rearrange("p t n -> p (t n)"), wc_sb[:], two_members, start=(h == 0), stop=(h == 1))
         hid_ps = psum.tile([P, EDGES], F32, name="hid_ps")
         for t in range(MEMBERS):
             member = nodes[:].indirect(offsets[:, t * LIST_COLUMNS : (t + 1) * LIST_COLUMNS])

@@ -1,5 +1,4 @@
 import concourse.mybir as mybir
-from concourse.masks import make_identity
 
 P = 128
 NODES = 512
@@ -35,13 +34,18 @@ def tile_hypergraphcompressor_kernel(tc, table, w1, b1, wc, offs, out):
         b1_sb = held.tile([P, 1], F32, name="b1_sb")
         nc.scalar.dma_start(b1_sb[:], b1)
 
+        ones = held.tile([P, P], F32, name="ones")
+        nc.vector.memset(ones[:], 1.0)
+        columns = held.tile([P, P], BF16, name="columns")
+        nc.vector.tensor_tensor_scan(columns[:], ones[:], ones[:], 0.0, mybir.AluOpType.mult, mybir.AluOpType.add)
+        share = held.tile([P, 2], BF16, name="share")
+        nc.vector.memset(share[:], 1.0 / P)
+        partitions = psum.tile([P, 2], F32, name="partitions")
+        nc.tensor.matmul(partitions[:], columns[:], share[:], start=True, stop=True)
         identity = held.tile([P, P], BF16, name="identity")
-        zero = held.tile([P, 1], F32, name="zero")
-        nc.vector.memset(zero[:], 0.0)
-        nc.vector.memset(identity[:], 0.0)
-        make_identity(nc, identity[:], nomemset=True)
+        nc.vector.tensor_scalar(identity[:], columns[:], partitions[:, 0:1], None, mybir.AluOpType.is_equal)
         early = held.tile([P, 1], F32, name="early")
-        nc.scalar.activation(early[:], zero[:], mybir.ActivationFunctionType.Relu)
+        nc.scalar.activation(early[:], ones[:, 0:1], mybir.ActivationFunctionType.Relu)
         nodes = held.tile([P, NODES], BF16, name="nodes")
         for c in range(BLOCKS):
             flipped = psum.tile([P, P], BF16, name="flipped%d" % c)

import concourse.mybir as mybir

P = 128
NODES = 512
MEMBERS = 4
EDGES = 64
BLOCKS = NODES // P
LIST_COLUMNS = EDGES // 16

BF16, F32, U16 = mybir.dt.bfloat16, mybir.dt.float32, mybir.dt.uint16

FLOPS = 2 * (2 * P * P * MEMBERS * EDGES)


def tile_hypergraphcompressor_kernel(tc, table, w1, b1, wc, offs, out):
    nc = tc.nc
    with (
        tc.tile_pool(name="held", bufs=1) as held,
        tc.psum_pool(name="psum", bufs=1) as psum,
    ):
        rows = held.tile([P, BLOCKS, P], BF16, name="rows")
        blocks = table.rearrange("(c p) f -> p c f", p=P)
        half = BLOCKS // 2
        nc.sync.dma_start(rows[:, 0:half, :], blocks[:, 0:half, :])
        nc.scalar.dma_start(rows[:, half:BLOCKS, :], blocks[:, half:BLOCKS, :])

        offsets = held.tile([P, MEMBERS * LIST_COLUMNS], U16, name="offsets")
        nc.sync.dma_start(offsets[:], offs)

        wc_sb = held.tile([P, P], BF16, name="wc_sb")
        nc.scalar.dma_start(wc_sb[:], wc)
        w1_sb = held.tile([P, MEMBERS, P], BF16, name="w1_sb")
        nc.sync.dma_start(w1_sb[:], w1.rearrange("(t f) d -> f t d", f=P))
        b1_sb = held.tile([P, 1], F32, name="b1_sb")
        nc.scalar.dma_start(b1_sb[:], b1)

        ones = held.tile([P, P], F32, name="ones")
        nc.vector.memset(ones[:], 1.0)
        columns = held.tile([P, P], BF16, name="columns")
        nc.vector.tensor_tensor_scan(columns[:], ones[:], ones[:], 0.0, mybir.AluOpType.mult, mybir.AluOpType.add)
        share = held.tile([P, 2], BF16, name="share")
        nc.vector.memset(share[:], 1.0 / P)
        partitions = psum.tile([P, 2], F32, name="partitions")
        nc.tensor.matmul(partitions[:], columns[:], share[:], start=True, stop=True)
        identity = held.tile([P, P], BF16, name="identity")
        nc.vector.tensor_scalar(identity[:], columns[:], partitions[:, 0:1], None, mybir.AluOpType.is_equal)
        early = held.tile([P, 1], F32, name="early")
        nc.scalar.activation(early[:], ones[:, 0:1], mybir.ActivationFunctionType.Relu)
        nodes = held.tile([P, NODES], BF16, name="nodes")
        for c in range(BLOCKS):
            flipped = psum.tile([P, P], BF16, name="flipped%d" % c)
            nc.tensor.transpose(flipped[:], rows[:, c, :], identity[:])
            nc.vector.tensor_copy(nodes[:, c * P : (c + 1) * P], flipped[:])

        edge_ps = psum.tile([P, 2, EDGES], F32, name="edge_ps")
        for h in range(2):
            two_members = nodes[:].indirect(offsets[:, 2 * h * LIST_COLUMNS : 2 * (h + 1) * LIST_COLUMNS])
            nc.tensor.matmul(edge_ps[:].rearrange("p t n -> p (t n)"), wc_sb[:], two_members, start=(h == 0), stop=(h == 1))
        hid_ps = psum.tile([P, EDGES], F32, name="hid_ps")
        for t in range(MEMBERS):
            member = nodes[:].indirect(offsets[:, t * LIST_COLUMNS : (t + 1) * LIST_COLUMNS])
            nc.tensor.matmul(hid_ps[:], w1_sb[:, t, :], member, start=(t == 0), stop=(t == MEMBERS - 1))

        edge_sum = held.tile([P, EDGES], F32, name="edge_sum")
        nc.vector.tensor_reduce(edge_sum[:], edge_ps[:].rearrange("p t n -> p n t"), mybir.AxisListType.X, mybir.AluOpType.add)
        edge_sb = held.tile([P, EDGES], F32, name="edge_sb")
        nc.vector.tensor_scalar_mul(edge_sb[:], edge_sum[:], 1.0 / MEMBERS)
        nc.sync.dma_start(out[P : 2 * P, :], edge_sb[:])
        hid_sb = held.tile([P, EDGES], F32, name="hid_sb")
        nc.scalar.activation(hid_sb[:], hid_ps[:], mybir.ActivationFunctionType.Relu, bias=b1_sb[:])
        nc.scalar.dma_start(out[0:P, :], hid_sb[:])
